import numpy as np
import ml_dtypes


def mxq(x, axis, fmt="e4m3"):
    dtype, down = {"e4m3": (ml_dtypes.float8_e4m3fn, 7), "e5m2": (ml_dtypes.float8_e5m2, 14)}[fmt]
    v = np.moveaxis(np.asarray(x, np.float32).astype(ml_dtypes.bfloat16).astype(np.float64), axis, -1)
    blocks = v.reshape(v.shape[:-1] + (-1, 32))
    amax = np.abs(blocks).max(-1, keepdims=True)
    byte = np.maximum(np.where(amax > 0, np.frexp(amax)[1] - 1 + 127, 0) - down, 1)
    scale = np.exp2(byte - 127.0)
    codes = (blocks / scale).astype(np.float32).astype(dtype).astype(np.float64)
    return np.moveaxis((codes * scale).reshape(v.shape), -1, axis)


WIDE = False


def mx_kscale(k):
    if not WIDE:
        return np.ones(k)
    levels = np.array([10, -10, 5, -5, 0])
    a = np.random.permutation(np.resize(levels, k // 512 * 4)).reshape(k // 512, 4)
    idx = np.arange(k)
    return np.exp2(a[idx // 512, idx % 128 // 32])


BF16 = ml_dtypes.bfloat16


def bf(x):
    return np.asarray(x, np.float32).astype(BF16)


def f64(x):
    return np.asarray(x).astype(np.float64)


B, C, HID, H, W = 2, 512, 64, 16, 16
N_P, N_H, N_F, N_U, N_L = 7, 3, 2, 4, 2
EPS = 1e-5


def setup_inputs():
    s = mx_kscale(C)
    off = 0.5 * np.random.standard_normal((1, C, 1, 1))
    return {
        "p_nodes": bf(np.random.standard_normal((N_P, B, HID, H, W))),
        "h_nodes": bf(np.random.standard_normal((N_H, B, HID, H, W))),
        "f_nodes": bf(np.random.standard_normal((N_F, B, HID, H, W))),
        "xp": bf((np.random.standard_normal((B, C, H, W)) + off) * s[None, :, None, None]),
        "h_att": bf(np.random.uniform(0.0, 1.0, (N_H, B, 1, H, W))),
        "Wu": bf(np.random.standard_normal((N_U * HID, C)) / np.sqrt(C) / s[None, :]),
        "Wl": bf(np.random.standard_normal((N_L * HID, C)) / np.sqrt(C) / s[None, :]),
        "gamma_u": bf(1.0 + 0.1 * np.random.standard_normal(N_U * HID)),
        "beta_u": bf(0.1 * np.random.standard_normal(N_U * HID)),
        "gamma_l": bf(1.0 + 0.1 * np.random.standard_normal(N_L * HID)),
        "beta_l": bf(0.1 * np.random.standard_normal(N_L * HID)),
    }


def conv_bn_relu(x, Wc, gamma, beta):
    y = (mxq(Wc, 1, "e4m3") @ mxq(x, 1, "e4m3").reshape(B, C, H * W)).reshape(B, -1, H, W)
    m = y.mean(axis=(0, 2, 3), keepdims=True)
    v = y.var(axis=(0, 2, 3), keepdims=True)
    y = (y - m) / np.sqrt(v + EPS)
    y = y * gamma[None, :, None, None] + beta[None, :, None, None]
    return np.maximum(y, 0.0)


def reference(p_nodes, h_nodes, f_nodes, xp, h_att, Wu, Wl, gamma_u, beta_u, gamma_l, beta_l):
    p_nodes, h_nodes, xp, h_att = f64(p_nodes), f64(h_nodes), f64(xp), f64(h_att)
    du = conv_bn_relu(h_att[1] * xp, f64(Wu), f64(gamma_u), f64(beta_u))
    dl = conv_bn_relu(h_att[2] * xp, f64(Wl), f64(gamma_l), f64(beta_l))
    du4 = du.reshape(B, N_U, HID, H, W).transpose(1, 0, 2, 3, 4)
    dl2 = dl.reshape(B, N_L, HID, H, W).transpose(1, 0, 2, 3, 4)
    p0 = 0.5 * (h_nodes[0] + p_nodes[0])
    p_up = 0.5 * (p_nodes[1:1 + N_U] + du4)
    p_low = 0.5 * (p_nodes[1 + N_U:N_P] + dl2)
    return np.concatenate([p0[None], p_up, p_low], axis=0)

@@ -1,0 +1,220 @@
+from contextlib import ExitStack
+
+import concourse.mybir as mybir
+from concourse.masks import make_identity
+
+BF16 = mybir.dt.bfloat16
+F32 = mybir.dt.float32
+U32 = mybir.dt.uint32
+U8 = mybir.dt.uint8
+FP8X4 = mybir.dt.float8_e4m3fn_x4
+ALU = mybir.AluOpType
+ACT = mybir.ActivationFunctionType
+
+P = 128
+PACK = 4
+B, C, HID, PIX = 2, 512, 64, 256
+COLS = B * PIX
+N_U, N_L = 4, 2
+TILES = (N_U + N_L) * HID // P
+NODES_PER_TILE = P // HID
+ATT_RUN = COLS // P
+EPS = 1e-5
+
+FLOPS = 2 * (N_U + N_L) * HID * C * COLS
+BYTES = (
+    2 * (7 * COLS * HID + COLS * HID + C * COLS + 2 * COLS + (N_U + N_L) * HID * (C + 2))
+    + 4 * 7 * COLS * HID
+)
+
+
+def tile_gnn_s_kernel(
+    tc, p_nodes, h_nodes, f_nodes, xp, h_att, Wu, Wl, gamma_u, beta_u, gamma_l, beta_l, out
+):
+    nc = tc.nc
+    with ExitStack() as ctx:
+        keep = ctx.enter_context(tc.tile_pool(name="keep", bufs=1))
+        psum = ctx.enter_context(tc.psum_pool(name="psum", bufs=1))
+
+        att_cols = keep.tile([P, 2, ATT_RUN], BF16)
+        nc.sync.dma_start(
+            out=att_cols[:],
+            in_=h_att[1:3].rearrange("i b o y x -> i (b o y x)").rearrange("i (p m) -> p i m", m=ATT_RUN),
+        )
+        x_sb = keep.tile([P, B, PACK, PIX], BF16)
+        nc.sync.dma_start(
+            out=x_sb[:].rearrange("q b (u e) x -> q b u (e x)", u=2),
+            in_=xp.rearrange("b (u q e) y x -> q b u (e y x)", u=2, e=2),
+        )
+        w_sb = keep.tile([P, TILES, C], BF16)
+        nc.sync.dma_start(out=w_sb[:, 0:2, :], in_=Wu.rearrange("(t p) k -> p t k", p=P))
+        nc.sync.dma_start(out=w_sb[:, 2, :], in_=Wl)
+        p_sb = keep.tile([P, TILES, B, PIX], BF16)
+        for t in range(TILES):
+            for j in range(NODES_PER_TILE):
+                nc.sync.dma_start(
+                    out=p_sb[j * HID : (j + 1) * HID, t, :, :],
+                    in_=p_nodes[1 + NODES_PER_TILE * t + j].rearrange("b h y x -> h b (y x)"),
+                )
+        gb_rows = keep.tile([P, P], BF16)
+        nc.vector.memset(gb_rows[:], 0.0)
+        nc.scalar.dma_start(out=gb_rows[0:2, :], in_=gamma_u.rearrange("(t p) -> t p", p=P))
+        nc.scalar.dma_start(out=gb_rows[2:3, :], in_=gamma_l.rearrange("(t p) -> t p", p=P))
+        nc.scalar.dma_start(out=gb_rows[3:5, :], in_=beta_u.rearrange("(t p) -> t p", p=P))
+        nc.scalar.dma_start(out=gb_rows[5:6, :], in_=beta_l.rearrange("(t p) -> t p", p=P))
+        p0_sb = keep.tile([P, PIX], BF16)
+        nc.scalar.dma_start(out=p0_sb[:], in_=p_nodes[0].rearrange("b h y x -> (b h) (y x)"))
+        h0_sb = keep.tile([P, PIX], BF16)
+        nc.scalar.dma_start(out=h0_sb[:], in_=h_nodes[0].rearrange("b h y x -> (b h) (y x)"))
+
+        ident_bf = keep.tile([P, P], BF16)
+        make_identity(nc, ident_bf[:])
+        ident_f32 = keep.tile([P, P], F32)
+        make_identity(nc, ident_f32[:])
+        eps = keep.tile([P, 1], F32)
+        nc.vector.memset(eps[:], EPS)
+        root_of_eps = keep.tile([P, 1], F32)
+        nc.scalar.activation(out=root_of_eps[:], in_=eps[:], func=ACT.Sqrt)
+
+        att_ps = []
+        for i in range(2):
+            att_i = psum.tile([P, ATT_RUN, P], BF16, name="att_ps%d" % i)
+            for m in range(ATT_RUN):
+                nc.tensor.transpose(
+                    out=att_i[:, m, :],
+                    in_=att_cols[:, i, m : m + 1].to_broadcast([P, P]),
+                    identity=ident_bf[:],
+                )
+            att_ps.append(att_i)
+
+        w_grouped = keep.tile([P, TILES, P, PACK], BF16, align_bytes=64)
+        w_codes = keep.tile([P, TILES, P], U32, align_bytes=64)
+        w_scales = keep.tile([P, TILES, P], U8, align_bytes=64)
+        w_banks = ((0, 2), (2, 3))
+        for first, end in w_banks:
+            blocks = slice(first, end)
+            wT_ps = psum.tile([P, end - first, 2, P], F32, name="wT_ps%d" % first)
+            for t in range(first, end):
+                words = w_sb[:, t, :].bitcast(F32)
+                for u in range(2):
+                    nc.tensor.transpose(
+                        out=wT_ps[:, t - first, u, :],
+                        in_=words[:, u * P : (u + 1) * P],
+                        identity=ident_f32[:],
+                    )
+            nc.scalar.copy(
+                out=w_grouped[:, blocks].rearrange("q k o t -> q k (o t)").bitcast(F32).rearrange(
+                    "q k (o u) -> q k o u", u=2
+                ),
+                in_=wT_ps[:].rearrange("q k u o -> q k o u"),
+            )
+
+        gbT_ps = psum.tile([P, P], BF16)
+        nc.tensor.transpose(out=gbT_ps[:], in_=gb_rows[:], identity=ident_bf[:])
+        half_gb = keep.tile([P, 2, TILES], F32)
+        nc.scalar.mul(
+            out=half_gb[:].rearrange("p g t -> p (g t)"), in_=gbT_ps[:, 0 : 2 * TILES], mul=0.5
+        )
+        minus_half_gamma = keep.tile([P, TILES], F32)
+        nc.scalar.mul(out=minus_half_gamma[:], in_=gbT_ps[:, 0:TILES], mul=-0.5)
+
+        o0_sb = keep.tile([P, PIX], F32)
+        nc.gpsimd.tensor_tensor(out=o0_sb[:], in0=p0_sb[:], in1=h0_sb[:], op=ALU.add)
+        nc.scalar.mul(out=o0_sb[:], in_=o0_sb[:], mul=0.5)
+        nc.sync.dma_start(out=out[0].rearrange("b h y x -> (b h) (y x)"), in_=o0_sb[:])
+
+        tiles_of = ((0, 1), (2,))
+        x_grouped = [keep.tile([P, COLS, PACK], BF16, align_bytes=64, name="x_grouped%d" % i) for i in range(2)]
+        x_codes = [keep.tile([P, COLS], U32, align_bytes=64, name="x_codes%d" % i) for i in range(2)]
+        x_scales = [keep.tile([P, COLS], U8, align_bytes=64, name="x_scales%d" % i) for i in range(2)]
+        y_ps = [psum.tile([P, COLS], F32, name="y_ps%d" % t) for t in range(TILES)]
+
+        def multiply(i):
+            nc.vector.tensor_tensor(
+                out=x_grouped[i][:].rearrange("q (b a m) t -> q b a m t", b=B, m=ATT_RUN),
+                in0=x_sb[:].rearrange("q b t (a m) -> q b a m t", m=ATT_RUN),
+                in1=att_ps[i][:]
+                .rearrange("q m (b a) -> q b a m", b=B)
+                .unsqueeze(4)
+                .to_broadcast([P, B, PIX // ATT_RUN, ATT_RUN, PACK]),
+                op=ALU.mult,
+            )
+
+        def convolve(i):
+            nc.vector.quantize_mx(
+                out=x_codes[i][:].bitcast(FP8X4),
+                scales=x_scales[i][:],
+                in_=x_grouped[i][:].rearrange("q w t -> q (w t)"),
+            )
+            for t in tiles_of[i]:
+                nc.tensor.matmul_mx(
+                    out=y_ps[t][:],
+                    lhsT=w_codes[:, t, :].bitcast(FP8X4),
+                    lhsT_scale=w_scales[:, t, :],
+                    rhs=x_codes[i][:].bitcast(FP8X4),
+                    rhs_scale=x_scales[i][:],
+                    start=True,
+                    stop=True,
+                )
+
+        multiply(0)
+        for first, end in w_banks:
+            blocks = slice(first, end)
+            nc.vector.quantize_mx(
+                out=w_codes[:, blocks].rearrange("q k o -> q (k o)").bitcast(FP8X4),
+                scales=w_scales[:, blocks].rearrange("q k o -> q (k o)"),
+                in_=w_grouped[:, blocks].rearrange("q k o t -> q (k o t)"),
+            )
+        convolve(0)
+        multiply(1)
+        convolve(1)
+
+        stats = keep.tile([P, TILES, 6], F32)
+        mean_var = keep.tile([P, TILES, 2], F32)
+        std = keep.tile([P, TILES], F32)
+        rstd = keep.tile([P, TILES], F32)
+        minus_mean_gamma = keep.tile([P, TILES], F32)
+        scale = keep.tile([P, TILES], F32)
+        shift = keep.tile([P, TILES], F32)
+
+        for tiles in tiles_of:
+            cs = slice(tiles[0], tiles[-1] + 1)
+            for t in tiles:
+                nc.vector.bn_stats(out=stats[:, t, :], in_=y_ps[t][:])
+                nc.vector.bn_aggr(out=mean_var[:, t, :], in_=stats[:, t, :])
+            nc.scalar.activation(out=std[:, cs], in_=mean_var[:, cs, 1], func=ACT.Sqrt, bias=eps[:])
+            nc.vector.tensor_tensor(
+                out=minus_mean_gamma[:, cs], in0=mean_var[:, cs, 0], in1=minus_half_gamma[:, cs], op=ALU.mult
+            )
+        for tiles in tiles_of:
+            cs = slice(tiles[0], tiles[-1] + 1)
+            nc.vector.reciprocal(out=rstd[:, cs], in_=std[:, cs])
+            nc.vector.tensor_tensor(out=scale[:, cs], in0=rstd[:, cs], in1=half_gb[:, 0, cs], op=ALU.mult)
+            for t in tiles:
+                nc.vector.scalar_tensor_tensor(
+                    out=shift[:, t : t + 1],
+                    in0=minus_mean_gamma[:, t : t + 1],
+                    scalar=rstd[:, t : t + 1],
+                    in1=half_gb[:, 1, t : t + 1],
+                    op0=ALU.mult,
+                    op1=ALU.add,
+                )
+        for t in range(TILES):
+            z_sb = keep.tile([P, COLS], F32, name="z_sb%d" % t)
+            nc.scalar.activation(
+                out=z_sb[:], in_=y_ps[t][:], func=ACT.Relu, bias=shift[:, t : t + 1], scale=scale[:, t : t + 1]
+            )
+            o_sb = keep.tile([P, B, PIX], F32, name="o_sb%d" % t)
+            nc.vector.scalar_tensor_tensor(
+                out=o_sb[:].rearrange("p b x -> p (b x)"),
+                in0=p_sb[:, t].rearrange("p b x -> p (b x)"),
+                scalar=0.5,
+                in1=z_sb[:],
+                op0=ALU.mult,
+                op1=ALU.add,
+            )
+            for j in range(NODES_PER_TILE):
+                nc.sync.dma_start(
+                    out=out[1 + NODES_PER_TILE * t + j].rearrange("b h y x -> h b (y x)"),
+                    in_=o_sb[j * HID : (j + 1) * HID, :, :],
+                )

@@ -18,7 +18,8 @@ COLS = B * PIX
 N_U, N_L = 4, 2
 TILES = (N_U + N_L) * HID // P
 NODES_PER_TILE = P // HID
-ATT_RUN = COLS // P
+PAIR = 2
+ATT_RUN = COLS * PAIR // P
 EPS = 1e-5
 
 FLOPS = 2 * (N_U + N_L) * HID * C * COLS
@@ -33,19 +34,22 @@ def tile_gnn_s_kernel(
 ):
     nc = tc.nc
     with ExitStack() as ctx:
+        ctx.enter_context(tc.manual_schedule())
         keep = ctx.enter_context(tc.tile_pool(name="keep", bufs=1))
         psum = ctx.enter_context(tc.psum_pool(name="psum", bufs=1))
 
         att_cols = keep.tile([P, 2, ATT_RUN], BF16)
-        nc.sync.dma_start(
-            out=att_cols[:],
-            in_=h_att[1:3].rearrange("i b o y x -> i (b o y x)").rearrange("i (p m) -> p i m", m=ATT_RUN),
-        )
+        for e in range(PAIR):
+            nc.sync.dma_start(
+                out=att_cols[e:P:PAIR, :, :],
+                in_=h_att[1:3].rearrange("i b o y x -> i (b o y x)").rearrange("i (a m) -> a i m", m=ATT_RUN),
+            )
         x_sb = keep.tile([P, B, PACK, PIX], BF16)
-        nc.sync.dma_start(
-            out=x_sb[:].rearrange("q b (u e) x -> q b u (e x)", u=2),
-            in_=xp.rearrange("b (u q e) y x -> q b u (e y x)", u=2, e=2),
-        )
+        for b in range(B):
+            nc.sync.dma_start(
+                out=x_sb[:, b].rearrange("q (u e) x -> q u (e x)", u=2),
+                in_=xp[b].rearrange("(u q e) y x -> q u (e y x)", u=2, e=2),
+            )
         w_sb = keep.tile([P, TILES, C], BF16)
         nc.sync.dma_start(out=w_sb[:, 0:2, :], in_=Wu.rearrange("(t p) k -> p t k", p=P))
         nc.sync.dma_start(out=w_sb[:, 2, :], in_=Wl)
@@ -73,19 +77,27 @@ def tile_gnn_s_kernel(
         make_identity(nc, ident_f32[:])
         eps = keep.tile([P, 1], F32)
         nc.vector.memset(eps[:], EPS)
-        root_of_eps = keep.tile([P, 1], F32)
-        nc.scalar.activation(out=root_of_eps[:], in_=eps[:], func=ACT.Sqrt)
+        first_call = keep.tile([P, 1], F32)
+        nc.scalar.activation(out=first_call[:], in_=eps[:], func=ACT.Abs_reciprocal_sqrt)
 
-        att_ps = []
-        for i in range(2):
-            att_i = psum.tile([P, ATT_RUN, P], BF16, name="att_ps%d" % i)
+        xp_grouped = keep.tile([P, COLS, PACK], BF16)
+        for b in range(B):
+            nc.vector.tensor_copy(
+                out=xp_grouped[:, b * PIX : (b + 1) * PIX, :].rearrange("q (c r) t -> q c t r", r=4),
+                in_=x_sb[:, b].rearrange("q t (c r) -> q c t r", r=4),
+            )
+
+        att_ps = [psum.tile([P, P // PAIR, ATT_RUN, PAIR], BF16, name="att_ps%d" % i) for i in range(2)]
+
+        def spread(i):
             for m in range(ATT_RUN):
                 nc.tensor.transpose(
-                    out=att_i[:, m, :],
+                    out=att_ps[i][:, :, m, :],
                     in_=att_cols[:, i, m : m + 1].to_broadcast([P, P]),
                     identity=ident_bf[:],
                 )
-            att_ps.append(att_i)
+
+        spread(0)
 
         w_grouped = keep.tile([P, TILES, P, PACK], BF16, align_bytes=64)
         w_codes = keep.tile([P, TILES, P], U32, align_bytes=64)
@@ -109,6 +121,8 @@ def tile_gnn_s_kernel(
                 in_=wT_ps[:].rearrange("q k u o -> q k o u"),
             )
 
+        spread(1)
+
         gbT_ps = psum.tile([P, P], BF16)
         nc.tensor.transpose(out=gbT_ps[:], in_=gb_rows[:], identity=ident_bf[:])
         half_gb = keep.tile([P, 2, TILES], F32)
@@ -131,12 +145,12 @@ def tile_gnn_s_kernel(
 
         def multiply(i):
             nc.vector.tensor_tensor(
-                out=x_grouped[i][:].rearrange("q (b a m) t -> q b a m t", b=B, m=ATT_RUN),
-                in0=x_sb[:].rearrange("q b t (a m) -> q b a m t", m=ATT_RUN),
+                out=x_grouped[i][:].rearrange("q w (u e) -> q w u e", e=PAIR),
+                in0=xp_grouped[:].rearrange("q w (u e) -> q w u e", e=PAIR),
                 in1=att_ps[i][:]
-                .rearrange("q m (b a) -> q b a m", b=B)
-                .unsqueeze(4)
-                .to_broadcast([P, B, PIX // ATT_RUN, ATT_RUN, PACK]),
+                .rearrange("q a m e -> q (a m) e")
+                .unsqueeze(2)
+                .to_broadcast([P, COLS, PACK // PAIR, PAIR]),
                 op=ALU.mult,
             )
 
@@ -157,6 +171,65 @@ def tile_gnn_s_kernel(
                     stop=True,
                 )
 
+        stats = keep.tile([P, TILES, 6], F32)
+        mean_var = keep.tile([P, TILES, 2], F32)
+        minus_mean_gamma = keep.tile([P, TILES], F32)
+        rstd = keep.tile([P, TILES], F32)
+        scale = keep.tile([P, TILES], F32)
+        shift = keep.tile([P, TILES], F32)
+        z_sb = [keep.tile([P, B, PIX], F32, name="z_sb%d" % t) for t in range(TILES)]
+        o_sb = [keep.tile([P, B, PIX], F32, name="o_sb%d" % t) for t in range(TILES)]
+
+        def root(tiles):
+            for t in tiles:
+                nc.scalar.activation(
+                    out=minus_mean_gamma[:, t : t + 1],
+                    in_=mean_var[:, t, 0:1],
+                    func=ACT.Copy,
+                    scale=minus_half_gamma[:, t : t + 1],
+                )
+            cs = slice(tiles[0], tiles[-1] + 1)
+            nc.scalar.activation(
+                out=rstd[:, cs], in_=mean_var[:, cs, 1], func=ACT.Abs_reciprocal_sqrt, bias=eps[:]
+            )
+
+        def affine(t):
+            nc.scalar.activation(
+                out=scale[:, t : t + 1], in_=rstd[:, t : t + 1], func=ACT.Copy, scale=half_gb[:, 0, t : t + 1]
+            )
+            nc.scalar.activation(
+                out=shift[:, t : t + 1],
+                in_=minus_mean_gamma[:, t : t + 1],
+                func=ACT.Identity,
+                scale=rstd[:, t : t + 1],
+                bias=half_gb[:, 1, t : t + 1],
+            )
+
+        def relu(t, images):
+            nc.scalar.activation(
+                out=z_sb[t][:, images, :],
+                in_=y_ps[t][:].rearrange("p (b x) -> p b x", b=B)[:, images, :],
+                func=ACT.Relu,
+                bias=shift[:, t : t + 1],
+                scale=scale[:, t : t + 1],
+            )
+
+        def average(t, images):
+            nc.vector.scalar_tensor_tensor(
+                out=o_sb[t][:, images, :],
+                in0=p_sb[:, t, images, :],
+                scalar=0.5,
+                in1=z_sb[t][:, images, :],
+                op0=ALU.mult,
+                op1=ALU.add,
+            )
+            for j in range(NODES_PER_TILE):
+                nc.sync.dma_start(
+                    out=out[1 + NODES_PER_TILE * t + j].rearrange("b h y x -> h b (y x)")[:, images, :],
+                    in_=o_sb[t][j * HID : (j + 1) * HID, images, :],
+                )
+
+        both = slice(0, B)
         multiply(0)
         for first, end in w_banks:
             blocks = slice(first, end)
@@ -167,54 +240,23 @@ def tile_gnn_s_kernel(
             )
         convolve(0)
         multiply(1)
+        nc.vector.bn_stats(out=stats[:, 0, :], in_=y_ps[0][:])
         convolve(1)
-
-        stats = keep.tile([P, TILES, 6], F32)
-        mean_var = keep.tile([P, TILES, 2], F32)
-        std = keep.tile([P, TILES], F32)
-        rstd = keep.tile([P, TILES], F32)
-        minus_mean_gamma = keep.tile([P, TILES], F32)
-        scale = keep.tile([P, TILES], F32)
-        shift = keep.tile([P, TILES], F32)
-
-        for tiles in tiles_of:
-            cs = slice(tiles[0], tiles[-1] + 1)
-            for t in tiles:
-                nc.vector.bn_stats(out=stats[:, t, :], in_=y_ps[t][:])
-                nc.vector.bn_aggr(out=mean_var[:, t, :], in_=stats[:, t, :])
-            nc.scalar.activation(out=std[:, cs], in_=mean_var[:, cs, 1], func=ACT.Sqrt, bias=eps[:])
-            nc.vector.tensor_tensor(
-                out=minus_mean_gamma[:, cs], in0=mean_var[:, cs, 0], in1=minus_half_gamma[:, cs], op=ALU.mult
-            )
-        for tiles in tiles_of:
-            cs = slice(tiles[0], tiles[-1] + 1)
-            nc.vector.reciprocal(out=rstd[:, cs], in_=std[:, cs])
-            nc.vector.tensor_tensor(out=scale[:, cs], in0=rstd[:, cs], in1=half_gb[:, 0, cs], op=ALU.mult)
-            for t in tiles:
-                nc.vector.scalar_tensor_tensor(
-                    out=shift[:, t : t + 1],
-                    in0=minus_mean_gamma[:, t : t + 1],
-                    scalar=rstd[:, t : t + 1],
-                    in1=half_gb[:, 1, t : t + 1],
-                    op0=ALU.mult,
-                    op1=ALU.add,
-                )
-        for t in range(TILES):
-            z_sb = keep.tile([P, COLS], F32, name="z_sb%d" % t)
-            nc.scalar.activation(
-                out=z_sb[:], in_=y_ps[t][:], func=ACT.Relu, bias=shift[:, t : t + 1], scale=scale[:, t : t + 1]
-            )
-            o_sb = keep.tile([P, B, PIX], F32, name="o_sb%d" % t)
-            nc.vector.scalar_tensor_tensor(
-                out=o_sb[:].rearrange("p b x -> p (b x)"),
-                in0=p_sb[:, t].rearrange("p b x -> p (b x)"),
-                scalar=0.5,
-                in1=z_sb[:],
-                op0=ALU.mult,
-                op1=ALU.add,
-            )
-            for j in range(NODES_PER_TILE):
-                nc.sync.dma_start(
-                    out=out[1 + NODES_PER_TILE * t + j].rearrange("b h y x -> h b (y x)"),
-                    in_=o_sb[j * HID : (j + 1) * HID, :, :],
-                )
+        nc.vector.bn_stats(out=stats[:, 1, :], in_=y_ps[1][:])
+        nc.vector.bn_aggr(out=mean_var[:, 0, :], in_=stats[:, 0, :])
+        nc.vector.bn_aggr(out=mean_var[:, 1, :], in_=stats[:, 1, :])
+        root((0, 1))
+        affine(0)
+        affine(1)
+        nc.vector.bn_stats(out=stats[:, 2, :], in_=y_ps[2][:])
+        nc.vector.bn_aggr(out=mean_var[:, 2, :], in_=stats[:, 2, :])
+        relu(0, both)
+        root((2,))
+        relu(1, both)
+        affine(2)
+        average(0, both)
+        average(1, both)
+        for b in range(B):
+            relu(2, slice(b, b + 1))
+        for b in range(B):
+            average(2, slice(b, b + 1))

@@ -53,28 +53,33 @@ def tile_gnn_s_kernel(
         w_sb = keep.tile([P, TILES, C], BF16)
         nc.sync.dma_start(out=w_sb[:, 0:2, :], in_=Wu.rearrange("(t p) k -> p t k", p=P))
         nc.sync.dma_start(out=w_sb[:, 2, :], in_=Wl)
+        gb_rows = keep.tile([P, P], BF16)
+        nc.vector.memset(gb_rows[:], 0.0)
+        nc.sync.dma_start(out=gb_rows[0:2, :], in_=gamma_u.rearrange("(t p) -> t p", p=P))
+        nc.sync.dma_start(out=gb_rows[2:3, :], in_=gamma_l.rearrange("(t p) -> t p", p=P))
+        nc.sync.dma_start(out=gb_rows[3:5, :], in_=beta_u.rearrange("(t p) -> t p", p=P))
+        nc.sync.dma_start(out=gb_rows[5:6, :], in_=beta_l.rearrange("(t p) -> t p", p=P))
+        p0_sb = keep.tile([P, PIX], BF16)
+        nc.sync.dma_start(out=p0_sb[:], in_=p_nodes[0].rearrange("b h y x -> (b h) (y x)"))
+        h0_sb = keep.tile([P, PIX], BF16)
+        nc.sync.dma_start(out=h0_sb[:], in_=h_nodes[0].rearrange("b h y x -> (b h) (y x)"))
         p_sb = keep.tile([P, TILES, B, PIX], BF16)
         for t in range(TILES):
             for j in range(NODES_PER_TILE):
                 nc.sync.dma_start(
-                    out=p_sb[j * HID : (j + 1) * HID, t, :, :],
+                    out=p_sb[j:P:NODES_PER_TILE, t, :, :],
                     in_=p_nodes[1 + NODES_PER_TILE * t + j].rearrange("b h y x -> h b (y x)"),
                 )
-        gb_rows = keep.tile([P, P], BF16)
-        nc.vector.memset(gb_rows[:], 0.0)
-        nc.scalar.dma_start(out=gb_rows[0:2, :], in_=gamma_u.rearrange("(t p) -> t p", p=P))
-        nc.scalar.dma_start(out=gb_rows[2:3, :], in_=gamma_l.rearrange("(t p) -> t p", p=P))
-        nc.scalar.dma_start(out=gb_rows[3:5, :], in_=beta_u.rearrange("(t p) -> t p", p=P))
-        nc.scalar.dma_start(out=gb_rows[5:6, :], in_=beta_l.rearrange("(t p) -> t p", p=P))
-        p0_sb = keep.tile([P, PIX], BF16)
-        nc.scalar.dma_start(out=p0_sb[:], in_=p_nodes[0].rearrange("b h y x -> (b h) (y x)"))
-        h0_sb = keep.tile([P, PIX], BF16)
-        nc.scalar.dma_start(out=h0_sb[:], in_=h_nodes[0].rearrange("b h y x -> (b h) (y x)"))
 
         ident_bf = keep.tile([P, P], BF16)
         make_identity(nc, ident_bf[:])
         ident_f32 = keep.tile([P, P], F32)
         make_identity(nc, ident_f32[:])
+        shuffle_f32 = keep.tile([P, P], F32)
+        nc.gpsimd.tensor_copy(
+            out=shuffle_f32[:].rearrange("p (h j) -> p h j", j=NODES_PER_TILE),
+            in_=ident_f32[:].rearrange("p (j h) -> p h j", j=NODES_PER_TILE),
+        )
         eps = keep.tile([P, 1], F32)
         nc.vector.memset(eps[:], EPS)
         first_call = keep.tile([P, 1], F32)
@@ -112,7 +117,7 @@ def tile_gnn_s_kernel(
                     nc.tensor.transpose(
                         out=wT_ps[:, t - first, u, :],
                         in_=words[:, u * P : (u + 1) * P],
-                        identity=ident_f32[:],
+                        identity=shuffle_f32[:],
                     )
             nc.scalar.copy(
                 out=w_grouped[:, blocks].rearrange("q k o t -> q k (o t)").bitcast(F32).rearrange(
@@ -123,8 +128,13 @@ def tile_gnn_s_kernel(
 
         spread(1)
 
+        gb_shuffled = keep.tile([P, P], BF16)
+        nc.gpsimd.tensor_copy(
+            out=gb_shuffled[:].rearrange("r (h j) -> r h j", j=NODES_PER_TILE),
+            in_=gb_rows[:].rearrange("r (j h) -> r h j", j=NODES_PER_TILE),
+        )
         gbT_ps = psum.tile([P, P], BF16)
-        nc.tensor.transpose(out=gbT_ps[:], in_=gb_rows[:], identity=ident_bf[:])
+        nc.tensor.transpose(out=gbT_ps[:], in_=gb_shuffled[:], identity=ident_bf[:])
         half_gb = keep.tile([P, 2, TILES], F32)
         nc.scalar.mul(
             out=half_gb[:].rearrange("p g t -> p (g t)"), in_=gbT_ps[:, 0 : 2 * TILES], mul=0.5
@@ -226,7 +236,7 @@ def tile_gnn_s_kernel(
             for j in range(NODES_PER_TILE):
                 nc.sync.dma_start(
                     out=out[1 + NODES_PER_TILE * t + j].rearrange("b h y x -> h b (y x)")[:, images, :],
-                    in_=o_sb[t][j * HID : (j + 1) * HID, images, :],
+                    in_=o_sb[t][j:P:NODES_PER_TILE, images, :],
                 )
 
         both = slice(0, B)

@@ -85,14 +85,38 @@ def tile_gnn_s_kernel(
         first_call = keep.tile([P, 1], F32)
         nc.scalar.activation(out=first_call[:], in_=eps[:], func=ACT.Abs_reciprocal_sqrt)
 
+        tiles_of = ((0, 1), (2,))
         xp_grouped = keep.tile([P, COLS, PACK], BF16)
-        for b in range(B):
+        att_ps = [psum.tile([P, P // PAIR, ATT_RUN, PAIR], BF16, name="att_ps%d" % i) for i in range(2)]
+        x_grouped = [keep.tile([P, COLS, PACK], BF16, align_bytes=64, name="x_grouped%d" % i) for i in range(2)]
+        x_codes = [keep.tile([P, COLS], U32, align_bytes=64, name="x_codes%d" % i) for i in range(2)]
+        x_scales = [keep.tile([P, COLS], U8, align_bytes=64, name="x_scales%d" % i) for i in range(2)]
+        wT_ps = [psum.tile([P, len(tiles), 2, P], F32, name="wT_ps%d" % i) for i, tiles in enumerate(tiles_of)]
+        w_grouped = keep.tile([P, TILES, P, PACK], BF16, align_bytes=64)
+        w_codes = keep.tile([P, TILES, P], U32, align_bytes=64)
+        w_scales = keep.tile([P, TILES, P], U8, align_bytes=64)
+        y_ps = [psum.tile([P, COLS], F32, name="y_ps%d" % t) for t in range(TILES)]
+        half_p = keep.tile([P, TILES, B, PIX], F32)
+        stats = keep.tile([P, TILES, 6], F32)
+        mean_var = keep.tile([P, TILES, 2], F32)
+        minus_mean_gamma = keep.tile([P, TILES], F32)
+        rstd = keep.tile([P, TILES], F32)
+        scale = keep.tile([P, TILES], F32)
+        shift = keep.tile([P, TILES], F32)
+        z_sb = [keep.tile([P, B, PIX], F32, name="z_sb%d" % t) for t in range(TILES)]
+        o_sb = [keep.tile([P, B, PIX], F32, name="o_sb%d" % t) for t in range(TILES)]
+
+        def columns(b):
+            return slice(b * PIX, (b + 1) * PIX)
+
+        def tile_range(i):
+            return slice(tiles_of[i][0], tiles_of[i][-1] + 1)
+
+        def regroup(b):
             nc.vector.tensor_copy(
-                out=xp_grouped[:, b * PIX : (b + 1) * PIX, :].rearrange("q (c r) t -> q c t r", r=4),
+                out=xp_grouped[:, columns(b), :].rearrange("q (c r) t -> q c t r", r=4),
                 in_=x_sb[:, b].rearrange("q t (c r) -> q c t r", r=4),
             )
-
-        att_ps = [psum.tile([P, P // PAIR, ATT_RUN, PAIR], BF16, name="att_ps%d" % i) for i in range(2)]
 
         def spread(i):
             for m in range(ATT_RUN):
@@ -102,31 +126,123 @@ def tile_gnn_s_kernel(
                     identity=ident_bf[:],
                 )
 
-        spread(0)
+        def multiply(i, b):
+            nc.vector.tensor_tensor(
+                out=x_grouped[i][:, columns(b), :].rearrange("q w (u e) -> q w u e", e=PAIR),
+                in0=xp_grouped[:, columns(b), :].rearrange("q w (u e) -> q w u e", e=PAIR),
+                in1=att_ps[i][:]
+                .rearrange("q a m e -> q (a m) e")[:, columns(b), :]
+                .unsqueeze(2)
+                .to_broadcast([P, PIX, PACK // PAIR, PAIR]),
+                op=ALU.mult,
+            )
 
-        w_grouped = keep.tile([P, TILES, P, PACK], BF16, align_bytes=64)
-        w_codes = keep.tile([P, TILES, P], U32, align_bytes=64)
-        w_scales = keep.tile([P, TILES, P], U8, align_bytes=64)
-        w_banks = ((0, 2), (2, 3))
-        for first, end in w_banks:
-            blocks = slice(first, end)
-            wT_ps = psum.tile([P, end - first, 2, P], F32, name="wT_ps%d" % first)
-            for t in range(first, end):
+        def quantise_x(i, b):
+            nc.vector.quantize_mx(
+                out=x_codes[i][:, columns(b)].bitcast(FP8X4),
+                scales=x_scales[i][:, columns(b)],
+                in_=x_grouped[i][:, columns(b), :].rearrange("q w t -> q (w t)"),
+            )
+
+        def transpose_weights(i):
+            for k, t in enumerate(tiles_of[i]):
                 words = w_sb[:, t, :].bitcast(F32)
                 for u in range(2):
                     nc.tensor.transpose(
-                        out=wT_ps[:, t - first, u, :],
-                        in_=words[:, u * P : (u + 1) * P],
-                        identity=shuffle_f32[:],
+                        out=wT_ps[i][:, k, u, :], in_=words[:, u * P : (u + 1) * P], identity=shuffle_f32[:]
                     )
             nc.scalar.copy(
-                out=w_grouped[:, blocks].rearrange("q k o t -> q k (o t)").bitcast(F32).rearrange(
-                    "q k (o u) -> q k o u", u=2
-                ),
-                in_=wT_ps[:].rearrange("q k u o -> q k o u"),
+                out=w_grouped[:, tile_range(i)]
+                .rearrange("q k o t -> q k (o t)")
+                .bitcast(F32)
+                .rearrange("q k (o u) -> q k o u", u=2),
+                in_=wT_ps[i][:].rearrange("q k u o -> q k o u"),
             )
 
+        def quantise_weights(i):
+            nc.vector.quantize_mx(
+                out=w_codes[:, tile_range(i)].rearrange("q k o -> q (k o)").bitcast(FP8X4),
+                scales=w_scales[:, tile_range(i)].rearrange("q k o -> q (k o)"),
+                in_=w_grouped[:, tile_range(i)].rearrange("q k o t -> q (k o t)"),
+            )
+
+        def convolve(i):
+            for t in tiles_of[i]:
+                nc.tensor.matmul_mx(
+                    out=y_ps[t][:],
+                    lhsT=w_codes[:, t, :].bitcast(FP8X4),
+                    lhsT_scale=w_scales[:, t, :],
+                    rhs=x_codes[i][:].bitcast(FP8X4),
+                    rhs_scale=x_scales[i][:],
+                    start=True,
+                    stop=True,
+                )
+
+        def root(i):
+            for t in tiles_of[i]:
+                nc.scalar.activation(
+                    out=minus_mean_gamma[:, t : t + 1],
+                    in_=mean_var[:, t, 0:1],
+                    func=ACT.Copy,
+                    scale=minus_half_gamma[:, t : t + 1],
+                )
+            nc.scalar.activation(
+                out=rstd[:, tile_range(i)],
+                in_=mean_var[:, tile_range(i), 1],
+                func=ACT.Abs_reciprocal_sqrt,
+                bias=eps[:],
+            )
+
+        def scale_and_shift(t):
+            nc.scalar.activation(
+                out=scale[:, t : t + 1], in_=rstd[:, t : t + 1], func=ACT.Copy, scale=half_gb[:, 0, t : t + 1]
+            )
+            nc.scalar.activation(
+                out=shift[:, t : t + 1],
+                in_=minus_mean_gamma[:, t : t + 1],
+                func=ACT.Identity,
+                scale=rstd[:, t : t + 1],
+                bias=half_gb[:, 1, t : t + 1],
+            )
+
+        def normalise_on_scalar(t, images):
+            nc.scalar.activation(
+                out=z_sb[t][:, images, :],
+                in_=y_ps[t][:].rearrange("p (b x) -> p b x", b=B)[:, images, :],
+                func=ACT.Identity,
+                bias=shift[:, t : t + 1],
+                scale=scale[:, t : t + 1],
+            )
+
+        def normalise_on_vector(t):
+            nc.vector.tensor_scalar(
+                out=z_sb[t][:].rearrange("p b x -> p (b x)"),
+                in0=y_ps[t][:],
+                scalar1=scale[:, t : t + 1],
+                scalar2=shift[:, t : t + 1],
+                op0=ALU.mult,
+                op1=ALU.add,
+            )
+
+        def relu_average_store(t, images):
+            nc.vector.scalar_tensor_tensor(
+                out=o_sb[t][:, images, :],
+                in0=z_sb[t][:, images, :],
+                scalar=0.0,
+                in1=half_p[:, t, images, :],
+                op0=ALU.max,
+                op1=ALU.add,
+            )
+            for j in range(NODES_PER_TILE):
+                nc.sync.dma_start(
+                    out=out[1 + NODES_PER_TILE * t + j].rearrange("b h y x -> h b (y x)")[:, images, :],
+                    in_=o_sb[t][j:P:NODES_PER_TILE, images, :],
+                )
+
+        spread(0)
+        transpose_weights(0)
         spread(1)
+        transpose_weights(1)
 
         gb_shuffled = keep.tile([P, P], BF16)
         nc.gpsimd.tensor_copy(
@@ -141,132 +257,46 @@ def tile_gnn_s_kernel(
         )
         minus_half_gamma = keep.tile([P, TILES], F32)
         nc.scalar.mul(out=minus_half_gamma[:], in_=gbT_ps[:, 0:TILES], mul=-0.5)
-
         o0_sb = keep.tile([P, PIX], F32)
         nc.gpsimd.tensor_tensor(out=o0_sb[:], in0=p0_sb[:], in1=h0_sb[:], op=ALU.add)
         nc.scalar.mul(out=o0_sb[:], in_=o0_sb[:], mul=0.5)
         nc.sync.dma_start(out=out[0].rearrange("b h y x -> (b h) (y x)"), in_=o0_sb[:])
+        for t in range(TILES):
+            nc.scalar.mul(out=half_p[:, t], in_=p_sb[:, t], mul=0.5)
 
-        tiles_of = ((0, 1), (2,))
-        x_grouped = [keep.tile([P, COLS, PACK], BF16, align_bytes=64, name="x_grouped%d" % i) for i in range(2)]
-        x_codes = [keep.tile([P, COLS], U32, align_bytes=64, name="x_codes%d" % i) for i in range(2)]
-        x_scales = [keep.tile([P, COLS], U8, align_bytes=64, name="x_scales%d" % i) for i in range(2)]
-        y_ps = [psum.tile([P, COLS], F32, name="y_ps%d" % t) for t in range(TILES)]
-
-        def multiply(i):
-            nc.vector.tensor_tensor(
-                out=x_grouped[i][:].rearrange("q w (u e) -> q w u e", e=PAIR),
-                in0=xp_grouped[:].rearrange("q w (u e) -> q w u e", e=PAIR),
-                in1=att_ps[i][:]
-                .rearrange("q a m e -> q (a m) e")
-                .unsqueeze(2)
-                .to_broadcast([P, COLS, PACK // PAIR, PAIR]),
-                op=ALU.mult,
-            )
-
-        def convolve(i):
-            nc.vector.quantize_mx(
-                out=x_codes[i][:].bitcast(FP8X4),
-                scales=x_scales[i][:],
-                in_=x_grouped[i][:].rearrange("q w t -> q (w t)"),
-            )
-            for t in tiles_of[i]:
-                nc.tensor.matmul_mx(
-                    out=y_ps[t][:],
-                    lhsT=w_codes[:, t, :].bitcast(FP8X4),
-                    lhsT_scale=w_scales[:, t, :],
-                    rhs=x_codes[i][:].bitcast(FP8X4),
-                    rhs_scale=x_scales[i][:],
-                    start=True,
-                    stop=True,
-                )
-
-        stats = keep.tile([P, TILES, 6], F32)
-        mean_var = keep.tile([P, TILES, 2], F32)
-        minus_mean_gamma = keep.tile([P, TILES], F32)
-        rstd = keep.tile([P, TILES], F32)
-        scale = keep.tile([P, TILES], F32)
-        shift = keep.tile([P, TILES], F32)
-        z_sb = [keep.tile([P, B, PIX], F32, name="z_sb%d" % t) for t in range(TILES)]
-        o_sb = [keep.tile([P, B, PIX], F32, name="o_sb%d" % t) for t in range(TILES)]
-
-        def root(tiles):
-            for t in tiles:
-                nc.scalar.activation(
-                    out=minus_mean_gamma[:, t : t + 1],
-                    in_=mean_var[:, t, 0:1],
-                    func=ACT.Copy,
-                    scale=minus_half_gamma[:, t : t + 1],
-                )
-            cs = slice(tiles[0], tiles[-1] + 1)
-            nc.scalar.activation(
-                out=rstd[:, cs], in_=mean_var[:, cs, 1], func=ACT.Abs_reciprocal_sqrt, bias=eps[:]
-            )
-
-        def affine(t):
-            nc.scalar.activation(
-                out=scale[:, t : t + 1], in_=rstd[:, t : t + 1], func=ACT.Copy, scale=half_gb[:, 0, t : t + 1]
-            )
-            nc.scalar.activation(
-                out=shift[:, t : t + 1],
-                in_=minus_mean_gamma[:, t : t + 1],
-                func=ACT.Identity,
-                scale=rstd[:, t : t + 1],
-                bias=half_gb[:, 1, t : t + 1],
-            )
-
-        def relu(t, images):
-            nc.scalar.activation(
-                out=z_sb[t][:, images, :],
-                in_=y_ps[t][:].rearrange("p (b x) -> p b x", b=B)[:, images, :],
-                func=ACT.Relu,
-                bias=shift[:, t : t + 1],
-                scale=scale[:, t : t + 1],
-            )
-
-        def average(t, images):
-            nc.vector.scalar_tensor_tensor(
-                out=o_sb[t][:, images, :],
-                in0=p_sb[:, t, images, :],
-                scalar=0.5,
-                in1=z_sb[t][:, images, :],
-                op0=ALU.mult,
-                op1=ALU.add,
-            )
-            for j in range(NODES_PER_TILE):
-                nc.sync.dma_start(
-                    out=out[1 + NODES_PER_TILE * t + j].rearrange("b h y x -> h b (y x)")[:, images, :],
-                    in_=o_sb[t][j:P:NODES_PER_TILE, images, :],
-                )
+        for b in range(B):
+            regroup(b)
+        for b in range(B):
+            multiply(0, b)
+        for b in range(B):
+            quantise_x(0, b)
+        quantise_weights(0)
+        convolve(0)
+        for b in range(B):
+            multiply(1, b)
+        quantise_weights(1)
+        for b in range(B):
+            quantise_x(1, b)
+        convolve(1)
 
         both = slice(0, B)
-        multiply(0)
-        for first, end in w_banks:
-            blocks = slice(first, end)
-            nc.vector.quantize_mx(
-                out=w_codes[:, blocks].rearrange("q k o -> q (k o)").bitcast(FP8X4),
-                scales=w_scales[:, blocks].rearrange("q k o -> q (k o)"),
-                in_=w_grouped[:, blocks].rearrange("q k o t -> q (k o t)"),
-            )
-        convolve(0)
-        multiply(1)
-        nc.vector.bn_stats(out=stats[:, 0, :], in_=y_ps[0][:])
-        convolve(1)
-        nc.vector.bn_stats(out=stats[:, 1, :], in_=y_ps[1][:])
-        nc.vector.bn_aggr(out=mean_var[:, 0, :], in_=stats[:, 0, :])
-        nc.vector.bn_aggr(out=mean_var[:, 1, :], in_=stats[:, 1, :])
-        root((0, 1))
-        affine(0)
-        affine(1)
-        nc.vector.bn_stats(out=stats[:, 2, :], in_=y_ps[2][:])
-        nc.vector.bn_aggr(out=mean_var[:, 2, :], in_=stats[:, 2, :])
-        relu(0, both)
-        root((2,))
-        relu(1, both)
-        affine(2)
-        average(0, both)
-        average(1, both)
+        for t in tiles_of[0]:
+            nc.vector.bn_stats(out=stats[:, t, :], in_=y_ps[t][:])
+        for t in tiles_of[0]:
+            nc.vector.bn_aggr(out=mean_var[:, t, :], in_=stats[:, t, :])
+        root(0)
+        for t in tiles_of[0]:
+            scale_and_shift(t)
+        for t in tiles_of[1]:
+            nc.vector.bn_stats(out=stats[:, t, :], in_=y_ps[t][:])
+            nc.vector.bn_aggr(out=mean_var[:, t, :], in_=stats[:, t, :])
+        normalise_on_scalar(0, both)
+        normalise_on_vector(1)
+        root(1)
+        scale_and_shift(2)
+        relu_average_store(0, both)
+        relu_average_store(1, both)
         for b in range(B):
-            relu(2, slice(b, b + 1))
+            normalise_on_scalar(2, slice(b, b + 1))
         for b in range(B):
-            average(2, slice(b, b + 1))
+            relu_average_store(2, slice(b, b + 1))

@@ -19,7 +19,7 @@ N_U, N_L = 4, 2
 TILES = (N_U + N_L) * HID // P
 NODES_PER_TILE = P // HID
 PAIR = 2
-ATT_RUN = COLS * PAIR // P
+ATT_RUN = PIX * PAIR // P
 EPS = 1e-5
 
 FLOPS = 2 * (N_U + N_L) * HID * C * COLS
@@ -38,11 +38,11 @@ def tile_gnn_s_kernel(
         keep = ctx.enter_context(tc.tile_pool(name="keep", bufs=1))
         psum = ctx.enter_context(tc.psum_pool(name="psum", bufs=1))
 
-        att_cols = keep.tile([P, 2, ATT_RUN], BF16)
+        att_cols = keep.tile([P, 2 * B, ATT_RUN], BF16)
         for e in range(PAIR):
             nc.sync.dma_start(
                 out=att_cols[e:P:PAIR, :, :],
-                in_=h_att[1:3].rearrange("i b o y x -> i (b o y x)").rearrange("i (a m) -> a i m", m=ATT_RUN),
+                in_=h_att[1:3].rearrange("i b o y x -> (i b) (o y x)").rearrange("g (a m) -> a g m", m=ATT_RUN),
             )
         x_sb = keep.tile([P, B, PACK, PIX], BF16)
         for b in range(B):
@@ -87,7 +87,7 @@ def tile_gnn_s_kernel(
 
         tiles_of = ((0, 1), (2,))
         xp_grouped = keep.tile([P, COLS, PACK], BF16)
-        att_ps = [psum.tile([P, P // PAIR, ATT_RUN, PAIR], BF16, name="att_ps%d" % i) for i in range(2)]
+        att_ps = [psum.tile([P, 2, P // PAIR, ATT_RUN, PAIR], BF16, name="att_ps%d" % b) for b in range(B)]
         x_grouped = [keep.tile([P, COLS, PACK], BF16, align_bytes=64, name="x_grouped%d" % i) for i in range(2)]
         x_codes = [keep.tile([P, COLS], U32, align_bytes=64, name="x_codes%d" % i) for i in range(2)]
         x_scales = [keep.tile([P, COLS], U8, align_bytes=64, name="x_scales%d" % i) for i in range(2)]
@@ -96,7 +96,7 @@ def tile_gnn_s_kernel(
         w_codes = keep.tile([P, TILES, P], U32, align_bytes=64)
         w_scales = keep.tile([P, TILES, P], U8, align_bytes=64)
         y_ps = [psum.tile([P, COLS], F32, name="y_ps%d" % t) for t in range(TILES)]
-        half_p = keep.tile([P, TILES, B, PIX], F32)
+        half_p0 = keep.tile([P, B, PIX], F32)
         stats = keep.tile([P, TILES, 6], F32)
         mean_var = keep.tile([P, TILES, 2], F32)
         minus_mean_gamma = keep.tile([P, TILES], F32)
@@ -105,6 +105,11 @@ def tile_gnn_s_kernel(
         shift = keep.tile([P, TILES], F32)
         z_sb = [keep.tile([P, B, PIX], F32, name="z_sb%d" % t) for t in range(TILES)]
         o_sb = [keep.tile([P, B, PIX], F32, name="o_sb%d" % t) for t in range(TILES)]
+        y0_sb = keep.tile([P, COLS], F32)
+        squares = keep.tile([P, COLS], F32)
+        sum0 = keep.tile([P, 1], F32)
+        minus_mean0 = keep.tile([P, 1], F32)
+        sum_of_squares0 = keep.tile([P, 1], F32)
 
         def columns(b):
             return slice(b * PIX, (b + 1) * PIX)
@@ -112,26 +117,27 @@ def tile_gnn_s_kernel(
         def tile_range(i):
             return slice(tiles_of[i][0], tiles_of[i][-1] + 1)
 
-        def regroup(b):
-            nc.vector.tensor_copy(
+        def regroup(b, copy):
+            copy(
                 out=xp_grouped[:, columns(b), :].rearrange("q (c r) t -> q c t r", r=4),
                 in_=x_sb[:, b].rearrange("q t (c r) -> q c t r", r=4),
             )
 
-        def spread(i):
-            for m in range(ATT_RUN):
-                nc.tensor.transpose(
-                    out=att_ps[i][:, :, m, :],
-                    in_=att_cols[:, i, m : m + 1].to_broadcast([P, P]),
-                    identity=ident_bf[:],
-                )
+        def spread(b):
+            for i in range(2):
+                for m in range(ATT_RUN):
+                    nc.tensor.transpose(
+                        out=att_ps[b][:, i, :, m, :],
+                        in_=att_cols[:, B * i + b, m : m + 1].to_broadcast([P, P]),
+                        identity=ident_bf[:],
+                    )
 
         def multiply(i, b):
             nc.vector.tensor_tensor(
                 out=x_grouped[i][:, columns(b), :].rearrange("q w (u e) -> q w u e", e=PAIR),
                 in0=xp_grouped[:, columns(b), :].rearrange("q w (u e) -> q w u e", e=PAIR),
-                in1=att_ps[i][:]
-                .rearrange("q a m e -> q (a m) e")[:, columns(b), :]
+                in1=att_ps[b][:, i]
+                .rearrange("q a m e -> q (a m) e")
                 .unsqueeze(2)
                 .to_broadcast([P, PIX, PACK // PAIR, PAIR]),
                 op=ALU.mult,
@@ -178,19 +184,32 @@ def tile_gnn_s_kernel(
                     stop=True,
                 )
 
-        def root(i):
-            for t in tiles_of[i]:
-                nc.scalar.activation(
-                    out=minus_mean_gamma[:, t : t + 1],
-                    in_=mean_var[:, t, 0:1],
-                    func=ACT.Copy,
-                    scale=minus_half_gamma[:, t : t + 1],
-                )
+        def statistics_on_scalar():
+            nc.scalar.activation(out=y0_sb[:], in_=y_ps[0][:], func=ACT.Copy, accum_out=sum0[:])
+            nc.scalar.mul(out=minus_mean0[:], in_=sum0[:], mul=-1.0 / COLS)
             nc.scalar.activation(
-                out=rstd[:, tile_range(i)],
-                in_=mean_var[:, tile_range(i), 1],
+                out=squares[:], in_=y0_sb[:], func=ACT.Square, bias=minus_mean0[:], accum_out=sum_of_squares0[:]
+            )
+            nc.scalar.activation(
+                out=minus_mean_gamma[:, 0:1], in_=minus_mean0[:], func=ACT.Copy, scale=half_gb[:, 0, 0:1]
+            )
+            nc.scalar.activation(
+                out=rstd[:, 0:1],
+                in_=sum_of_squares0[:],
                 func=ACT.Abs_reciprocal_sqrt,
+                scale=1.0 / COLS,
                 bias=eps[:],
+            )
+
+        def root(t):
+            nc.scalar.activation(
+                out=rstd[:, t : t + 1], in_=mean_var[:, t, 1:2], func=ACT.Abs_reciprocal_sqrt, bias=eps[:]
+            )
+            nc.scalar.activation(
+                out=minus_mean_gamma[:, t : t + 1],
+                in_=mean_var[:, t, 0:1],
+                func=ACT.Copy,
+                scale=minus_half_gamma[:, t : t + 1],
             )
 
         def scale_and_shift(t):
@@ -209,7 +228,7 @@ def tile_gnn_s_kernel(
             nc.scalar.activation(
                 out=z_sb[t][:, images, :],
                 in_=y_ps[t][:].rearrange("p (b x) -> p b x", b=B)[:, images, :],
-                func=ACT.Identity,
+                func=ACT.Relu,
                 bias=shift[:, t : t + 1],
                 scale=scale[:, t : t + 1],
             )
@@ -217,31 +236,41 @@ def tile_gnn_s_kernel(
         def normalise_on_vector(t):
             nc.vector.tensor_scalar(
                 out=z_sb[t][:].rearrange("p b x -> p (b x)"),
-                in0=y_ps[t][:],
+                in0=y0_sb[:],
                 scalar1=scale[:, t : t + 1],
                 scalar2=shift[:, t : t + 1],
                 op0=ALU.mult,
                 op1=ALU.add,
             )
 
-        def relu_average_store(t, images):
-            nc.vector.scalar_tensor_tensor(
-                out=o_sb[t][:, images, :],
-                in0=z_sb[t][:, images, :],
-                scalar=0.0,
-                in1=half_p[:, t, images, :],
-                op0=ALU.max,
-                op1=ALU.add,
-            )
+        def store(t, images):
             for j in range(NODES_PER_TILE):
                 nc.sync.dma_start(
                     out=out[1 + NODES_PER_TILE * t + j].rearrange("b h y x -> h b (y x)")[:, images, :],
                     in_=o_sb[t][j:P:NODES_PER_TILE, images, :],
                 )
 
+        def relu_average_store(t):
+            nc.vector.scalar_tensor_tensor(
+                out=o_sb[t][:], in0=z_sb[t][:], scalar=0.0, in1=half_p0[:], op0=ALU.max, op1=ALU.add
+            )
+            store(t, slice(0, B))
+
+        def average_store(t, images):
+            nc.vector.scalar_tensor_tensor(
+                out=o_sb[t][:, images, :],
+                in0=p_sb[:, t, images, :],
+                scalar=0.5,
+                in1=z_sb[t][:, images, :],
+                op0=ALU.mult,
+                op1=ALU.add,
+            )
+            store(t, images)
+
+        regroup(1, nc.scalar.copy)
         spread(0)
-        transpose_weights(0)
         spread(1)
+        transpose_weights(0)
         transpose_weights(1)
 
         gb_shuffled = keep.tile([P, P], BF16)
@@ -261,42 +290,37 @@ def tile_gnn_s_kernel(
         nc.gpsimd.tensor_tensor(out=o0_sb[:], in0=p0_sb[:], in1=h0_sb[:], op=ALU.add)
         nc.scalar.mul(out=o0_sb[:], in_=o0_sb[:], mul=0.5)
         nc.sync.dma_start(out=out[0].rearrange("b h y x -> (b h) (y x)"), in_=o0_sb[:])
-        for t in range(TILES):
-            nc.scalar.mul(out=half_p[:, t], in_=p_sb[:, t], mul=0.5)
+        nc.scalar.mul(out=half_p0[:], in_=p_sb[:, 0], mul=0.5)
 
-        for b in range(B):
-            regroup(b)
-        for b in range(B):
-            multiply(0, b)
+        regroup(0, nc.vector.tensor_copy)
+        multiply(0, 0)
+        multiply(1, 0)
+        multiply(0, 1)
         for b in range(B):
             quantise_x(0, b)
         quantise_weights(0)
         convolve(0)
-        for b in range(B):
-            multiply(1, b)
+        statistics_on_scalar()
+        multiply(1, 1)
         quantise_weights(1)
         for b in range(B):
             quantise_x(1, b)
         convolve(1)
 
         both = slice(0, B)
-        for t in tiles_of[0]:
-            nc.vector.bn_stats(out=stats[:, t, :], in_=y_ps[t][:])
-        for t in tiles_of[0]:
-            nc.vector.bn_aggr(out=mean_var[:, t, :], in_=stats[:, t, :])
-        root(0)
-        for t in tiles_of[0]:
-            scale_and_shift(t)
-        for t in tiles_of[1]:
+        for t in (1, 2):
             nc.vector.bn_stats(out=stats[:, t, :], in_=y_ps[t][:])
             nc.vector.bn_aggr(out=mean_var[:, t, :], in_=stats[:, t, :])
-        normalise_on_scalar(0, both)
-        normalise_on_vector(1)
         root(1)
+        scale_and_shift(0)
+        scale_and_shift(1)
+        normalise_on_vector(0)
+        normalise_on_scalar(1, both)
+        root(2)
         scale_and_shift(2)
-        relu_average_store(0, both)
-        relu_average_store(1, both)
+        relu_average_store(0)
+        average_store(1, both)
         for b in range(B):
             normalise_on_scalar(2, slice(b, b + 1))
         for b in range(B):
-            relu_average_store(2, slice(b, b + 1))
+            average_store(2, slice(b, b + 1))

@@ -107,7 +107,6 @@ def tile_gnn_s_kernel(
         o_sb = [keep.tile([P, B, PIX], F32, name="o_sb%d" % t) for t in range(TILES)]
         y0_sb = keep.tile([P, COLS], F32)
         squares = keep.tile([P, COLS], F32)
-        sum0 = keep.tile([P, 1], F32)
         minus_mean0 = keep.tile([P, 1], F32)
         sum_of_squares0 = keep.tile([P, 1], F32)
 
@@ -117,11 +116,14 @@ def tile_gnn_s_kernel(
         def tile_range(i):
             return slice(tiles_of[i][0], tiles_of[i][-1] + 1)
 
-        def regroup(b, copy):
-            copy(
+        def regroup_on_vector(b):
+            nc.vector.tensor_copy(
                 out=xp_grouped[:, columns(b), :].rearrange("q (c r) t -> q c t r", r=4),
                 in_=x_sb[:, b].rearrange("q t (c r) -> q c t r", r=4),
             )
+
+        def regroup_on_scalar(b):
+            nc.scalar.copy(out=xp_grouped[:, columns(b), :], in_=x_sb[:, b].rearrange("q t x -> q x t"))
 
         def spread(b):
             for i in range(2):
@@ -185,10 +187,11 @@ def tile_gnn_s_kernel(
                 )
 
         def statistics_on_scalar():
-            nc.scalar.activation(out=y0_sb[:], in_=y_ps[0][:], func=ACT.Copy, accum_out=sum0[:])
-            nc.scalar.mul(out=minus_mean0[:], in_=sum0[:], mul=-1.0 / COLS)
             nc.scalar.activation(
-                out=squares[:], in_=y0_sb[:], func=ACT.Square, bias=minus_mean0[:], accum_out=sum_of_squares0[:]
+                out=y0_sb[:], in_=y_ps[0][:], func=ACT.Copy, scale=-1.0 / COLS, accum_out=minus_mean0[:]
+            )
+            nc.scalar.activation(
+                out=squares[:], in_=y_ps[0][:], func=ACT.Square, bias=minus_mean0[:], accum_out=sum_of_squares0[:]
             )
             nc.scalar.activation(
                 out=minus_mean_gamma[:, 0:1], in_=minus_mean0[:], func=ACT.Copy, scale=half_gb[:, 0, 0:1]
@@ -214,7 +217,10 @@ def tile_gnn_s_kernel(
 
         def scale_and_shift(t):
             nc.scalar.activation(
-                out=scale[:, t : t + 1], in_=rstd[:, t : t + 1], func=ACT.Copy, scale=half_gb[:, 0, t : t + 1]
+                out=scale[:, t : t + 1],
+                in_=rstd[:, t : t + 1],
+                func=ACT.Copy,
+                scale=gamma_for_y0_sb[:] if t == 0 else half_gb[:, 0, t : t + 1],
             )
             nc.scalar.activation(
                 out=shift[:, t : t + 1],
@@ -267,7 +273,7 @@ def tile_gnn_s_kernel(
             )
             store(t, images)
 
-        regroup(1, nc.scalar.copy)
+        regroup_on_scalar(1)
         spread(0)
         spread(1)
         transpose_weights(0)
@@ -286,13 +292,15 @@ def tile_gnn_s_kernel(
         )
         minus_half_gamma = keep.tile([P, TILES], F32)
         nc.scalar.mul(out=minus_half_gamma[:], in_=gbT_ps[:, 0:TILES], mul=-0.5)
+        gamma_for_y0_sb = keep.tile([P, 1], F32)
+        nc.scalar.mul(out=gamma_for_y0_sb[:], in_=gbT_ps[:, 0:1], mul=-0.5 * COLS)
         o0_sb = keep.tile([P, PIX], F32)
         nc.gpsimd.tensor_tensor(out=o0_sb[:], in0=p0_sb[:], in1=h0_sb[:], op=ALU.add)
         nc.scalar.mul(out=o0_sb[:], in_=o0_sb[:], mul=0.5)
         nc.sync.dma_start(out=out[0].rearrange("b h y x -> (b h) (y x)"), in_=o0_sb[:])
         nc.scalar.mul(out=half_p0[:], in_=p_sb[:, 0], mul=0.5)
 
-        regroup(0, nc.vector.tensor_copy)
+        regroup_on_vector(0)
         multiply(0, 0)
         multiply(1, 0)
         multiply(0, 1)
@@ -315,8 +323,8 @@ def tile_gnn_s_kernel(
         scale_and_shift(0)
         scale_and_shift(1)
         normalise_on_vector(0)
-        normalise_on_scalar(1, both)
         root(2)
+        normalise_on_scalar(1, both)
         scale_and_shift(2)
         relu_average_store(0)
         average_store(1, both)

@@ -95,9 +95,10 @@ def tile_gnn_s_kernel(
         w_grouped = keep.tile([P, TILES, P, PACK], BF16, align_bytes=64)
         w_codes = keep.tile([P, TILES, P], U32, align_bytes=64)
         w_scales = keep.tile([P, TILES, P], U8, align_bytes=64)
-        y_ps = [psum.tile([P, COLS], F32, name="y_ps%d" % t) for t in range(TILES)]
+        y_ps = [psum.tile([P, COLS], F32, name="y_ps%d" % t) for t in tiles_of[0]]
         half_p0 = keep.tile([P, B, PIX], F32)
-        stats = keep.tile([P, TILES, 6], F32)
+        stats1 = keep.tile([P, 6], F32)
+        stats2 = keep.tile([P, B, 6], F32)
         mean_var = keep.tile([P, TILES, 2], F32)
         minus_mean_gamma = keep.tile([P, TILES], F32)
         rstd = keep.tile([P, TILES], F32)
@@ -122,8 +123,19 @@ def tile_gnn_s_kernel(
                 in_=x_sb[:, b].rearrange("q t (c r) -> q c t r", r=4),
             )
 
-        def regroup_on_scalar(b):
-            nc.scalar.copy(out=xp_grouped[:, columns(b), :], in_=x_sb[:, b].rearrange("q t x -> q x t"))
+        def regroup_on_scalar_and_gpsimd(b):
+            half = PIX // 2
+            nc.scalar.copy(
+                out=xp_grouped[:, b * PIX : b * PIX + half, :], in_=x_sb[:, b, :, 0:half].rearrange("q t x -> q x t")
+            )
+            nc.gpsimd.tensor_scalar(
+                out=xp_grouped[:, b * PIX + half : (b + 1) * PIX, :],
+                in0=x_sb[:, b, :, half:PIX].rearrange("q t x -> q x t"),
+                scalar1=1.0,
+                scalar2=0.0,
+                op0=ALU.mult,
+                op1=ALU.add,
+            )
 
         def spread(b):
             for i in range(2):
@@ -174,17 +186,28 @@ def tile_gnn_s_kernel(
                 in_=w_grouped[:, tile_range(i)].rearrange("q k o t -> q (k o t)"),
             )
 
-        def convolve(i):
-            for t in tiles_of[i]:
+        def convolve_upper():
+            for t in tiles_of[0]:
                 nc.tensor.matmul_mx(
                     out=y_ps[t][:],
                     lhsT=w_codes[:, t, :].bitcast(FP8X4),
                     lhsT_scale=w_scales[:, t, :],
-                    rhs=x_codes[i][:].bitcast(FP8X4),
-                    rhs_scale=x_scales[i][:],
+                    rhs=x_codes[0][:].bitcast(FP8X4),
+                    rhs_scale=x_scales[0][:],
                     start=True,
                     stop=True,
                 )
+
+        def convolve_lower(b):
+            nc.tensor.matmul_mx(
+                out=y2_ps[b][:],
+                lhsT=w_codes[:, 2, :].bitcast(FP8X4),
+                lhsT_scale=w_scales[:, 2, :],
+                rhs=x_codes[1][:, columns(b)].bitcast(FP8X4),
+                rhs_scale=x_scales[1][:, columns(b)],
+                start=True,
+                stop=True,
+            )
 
         def statistics_on_scalar():
             nc.scalar.activation(
@@ -230,13 +253,9 @@ def tile_gnn_s_kernel(
                 bias=half_gb[:, 1, t : t + 1],
             )
 
-        def normalise_on_scalar(t, images):
+        def normalise_on_scalar(t, z, y):
             nc.scalar.activation(
-                out=z_sb[t][:, images, :],
-                in_=y_ps[t][:].rearrange("p (b x) -> p b x", b=B)[:, images, :],
-                func=ACT.Relu,
-                bias=shift[:, t : t + 1],
-                scale=scale[:, t : t + 1],
+                out=z, in_=y, func=ACT.Relu, bias=shift[:, t : t + 1], scale=scale[:, t : t + 1]
             )
 
         def normalise_on_vector(t):
@@ -273,7 +292,7 @@ def tile_gnn_s_kernel(
             )
             store(t, images)
 
-        regroup_on_scalar(1)
+        regroup_on_scalar_and_gpsimd(1)
         spread(0)
         spread(1)
         transpose_weights(0)
@@ -284,7 +303,7 @@ def tile_gnn_s_kernel(
             out=gb_shuffled[:].rearrange("r (h j) -> r h j", j=NODES_PER_TILE),
             in_=gb_rows[:].rearrange("r (j h) -> r h j", j=NODES_PER_TILE),
         )
-        gbT_ps = psum.tile([P, P], BF16)
+        gbT_ps = psum.tile([P, P], BF16, tag="small")
         nc.tensor.transpose(out=gbT_ps[:], in_=gb_shuffled[:], identity=ident_bf[:])
         half_gb = keep.tile([P, 2, TILES], F32)
         nc.scalar.mul(
@@ -300,6 +319,8 @@ def tile_gnn_s_kernel(
         nc.sync.dma_start(out=out[0].rearrange("b h y x -> (b h) (y x)"), in_=o0_sb[:])
         nc.scalar.mul(out=half_p0[:], in_=p_sb[:, 0], mul=0.5)
 
+        y2_ps = [psum.tile([P, PIX], F32, name="y2_ps0"), psum.tile([P, PIX], F32, tag="small", name="y2_ps1")]
+
         regroup_on_vector(0)
         multiply(0, 0)
         multiply(1, 0)
@@ -307,28 +328,30 @@ def tile_gnn_s_kernel(
         for b in range(B):
             quantise_x(0, b)
         quantise_weights(0)
-        convolve(0)
+        convolve_upper()
         statistics_on_scalar()
         multiply(1, 1)
         quantise_weights(1)
         for b in range(B):
             quantise_x(1, b)
-        convolve(1)
+            convolve_lower(b)
 
         both = slice(0, B)
-        for t in (1, 2):
-            nc.vector.bn_stats(out=stats[:, t, :], in_=y_ps[t][:])
-            nc.vector.bn_aggr(out=mean_var[:, t, :], in_=stats[:, t, :])
+        nc.vector.bn_stats(out=stats1[:], in_=y_ps[1][:])
+        nc.vector.bn_stats(out=stats2[:, 0, :], in_=y2_ps[0][:])
+        nc.vector.bn_aggr(out=mean_var[:, 1, :], in_=stats1[:])
+        nc.vector.bn_stats(out=stats2[:, 1, :], in_=y2_ps[1][:])
+        nc.vector.bn_aggr(out=mean_var[:, 2, :], in_=stats2[:].rearrange("p b s -> p (b s)"))
         root(1)
         scale_and_shift(0)
         scale_and_shift(1)
         normalise_on_vector(0)
         root(2)
-        normalise_on_scalar(1, both)
+        normalise_on_scalar(1, z_sb[1][:].rearrange("p b x -> p (b x)"), y_ps[1][:])
         scale_and_shift(2)
         relu_average_store(0)
         average_store(1, both)
         for b in range(B):
-            normalise_on_scalar(2, slice(b, b + 1))
+            normalise_on_scalar(2, z_sb[2][:, b, :], y2_ps[b][:])
         for b in range(B):
             average_store(2, slice(b, b + 1))

@@ -19,7 +19,7 @@ N_U, N_L = 4, 2
 TILES = (N_U + N_L) * HID // P
 NODES_PER_TILE = P // HID
 PAIR = 2
-ATT_RUN = PIX * PAIR // P
+ATT_RUN = COLS * PAIR // P
 EPS = 1e-5
 
 FLOPS = 2 * (N_U + N_L) * HID * C * COLS
@@ -38,11 +38,11 @@ def tile_gnn_s_kernel(
         keep = ctx.enter_context(tc.tile_pool(name="keep", bufs=1))
         psum = ctx.enter_context(tc.psum_pool(name="psum", bufs=1))
 
-        att_cols = keep.tile([P, 2 * B, ATT_RUN], BF16)
+        att_cols = keep.tile([P, 2, ATT_RUN], BF16)
         for e in range(PAIR):
             nc.sync.dma_start(
                 out=att_cols[e:P:PAIR, :, :],
-                in_=h_att[1:3].rearrange("i b o y x -> (i b) (o y x)").rearrange("g (a m) -> a g m", m=ATT_RUN),
+                in_=h_att[1:3].rearrange("i b o y x -> i (b o y x)").rearrange("i (a m) -> a i m", m=ATT_RUN),
             )
         x_sb = keep.tile([P, B, PACK, PIX], BF16)
         for b in range(B):
@@ -87,7 +87,7 @@ def tile_gnn_s_kernel(
 
         tiles_of = ((0, 1), (2,))
         xp_grouped = keep.tile([P, COLS, PACK], BF16)
-        att_ps = [psum.tile([P, 2, P // PAIR, ATT_RUN, PAIR], BF16, name="att_ps%d" % b) for b in range(B)]
+        att_ps = [psum.tile([P, P // PAIR, ATT_RUN, PAIR], BF16, name="att_ps%d" % i) for i in range(2)]
         x_grouped = [keep.tile([P, COLS, PACK], BF16, align_bytes=64, name="x_grouped%d" % i) for i in range(2)]
         x_codes = [keep.tile([P, COLS], U32, align_bytes=64, name="x_codes%d" % i) for i in range(2)]
         x_scales = [keep.tile([P, COLS], U8, align_bytes=64, name="x_scales%d" % i) for i in range(2)]
@@ -137,21 +137,20 @@ def tile_gnn_s_kernel(
                 op1=ALU.add,
             )
 
-        def spread(b):
-            for i in range(2):
-                for m in range(ATT_RUN):
-                    nc.tensor.transpose(
-                        out=att_ps[b][:, i, :, m, :],
-                        in_=att_cols[:, B * i + b, m : m + 1].to_broadcast([P, P]),
-                        identity=ident_bf[:],
-                    )
+        def spread(i):
+            for m in range(ATT_RUN):
+                nc.tensor.transpose(
+                    out=att_ps[i][:, :, m, :],
+                    in_=att_cols[:, i, m : m + 1].to_broadcast([P, P]),
+                    identity=ident_bf[:],
+                )
 
         def multiply(i, b):
             nc.vector.tensor_tensor(
                 out=x_grouped[i][:, columns(b), :].rearrange("q w (u e) -> q w u e", e=PAIR),
                 in0=xp_grouped[:, columns(b), :].rearrange("q w (u e) -> q w u e", e=PAIR),
-                in1=att_ps[b][:, i]
-                .rearrange("q a m e -> q (a m) e")
+                in1=att_ps[i][:]
+                .rearrange("q a m e -> q (a m) e")[:, columns(b), :]
                 .unsqueeze(2)
                 .to_broadcast([P, PIX, PACK // PAIR, PAIR]),
                 op=ALU.mult,

@@ -47,8 +47,8 @@ def tile_gnn_s_kernel(
         x_sb = keep.tile([P, B, PACK, PIX], BF16)
         for b in range(B):
             nc.sync.dma_start(
-                out=x_sb[:, b].rearrange("q (u e) x -> q u (e x)", u=2),
-                in_=xp[b].rearrange("(u q e) y x -> q u (e y x)", u=2, e=2),
+                out=x_sb[:, b].rearrange("q t x -> q (t x)"),
+                in_=xp[b].rearrange("(q t) y x -> q (t y x)", t=PACK),
             )
         w_sb = keep.tile([P, TILES, C], BF16)
         nc.sync.dma_start(out=w_sb[:, 0:2, :], in_=Wu.rearrange("(t p) k -> p t k", p=P))
@@ -168,7 +168,7 @@ def tile_gnn_s_kernel(
                 words = w_sb[:, t, :].bitcast(F32)
                 for u in range(2):
                     nc.tensor.transpose(
-                        out=wT_ps[i][:, k, u, :], in_=words[:, u * P : (u + 1) * P], identity=shuffle_f32[:]
+                        out=wT_ps[i][:, k, u, :], in_=words[:, u : 2 * P : 2], identity=shuffle_f32[:]
                     )
             nc.scalar.copy(
                 out=w_grouped[:, tile_range(i)]
@@ -268,8 +268,9 @@ def tile_gnn_s_kernel(
             )
 
         def store(t, images):
+            queues = (nc.sync, nc.scalar) if t == 2 else (nc.sync, nc.sync)
             for j in range(NODES_PER_TILE):
-                nc.sync.dma_start(
+                queues[j].dma_start(
                     out=out[1 + NODES_PER_TILE * t + j].rearrange("b h y x -> h b (y x)")[:, images, :],
                     in_=o_sb[t][j:P:NODES_PER_TILE, images, :],
                 )

from contextlib import ExitStack

import concourse.mybir as mybir
from concourse.masks import make_identity

BF16 = mybir.dt.bfloat16
F32 = mybir.dt.float32
U32 = mybir.dt.uint32
U8 = mybir.dt.uint8
FP8X4 = mybir.dt.float8_e4m3fn_x4
ALU = mybir.AluOpType
ACT = mybir.ActivationFunctionType

P = 128
PACK = 4
B, C, HID, PIX = 2, 512, 64, 256
COLS = B * PIX
N_U, N_L = 4, 2
TILES = (N_U + N_L) * HID // P
NODES_PER_TILE = P // HID
PAIR = 2
ATT_RUN = COLS * PAIR // P
EPS = 1e-5

FLOPS = 2 * (N_U + N_L) * HID * C * COLS
BYTES = (
    2 * (7 * COLS * HID + COLS * HID + C * COLS + 2 * COLS + (N_U + N_L) * HID * (C + 2))
    + 4 * 7 * COLS * HID
)


def tile_gnn_s_kernel(
    tc, p_nodes, h_nodes, f_nodes, xp, h_att, Wu, Wl, gamma_u, beta_u, gamma_l, beta_l, out
):
    nc = tc.nc
    with ExitStack() as ctx:
        ctx.enter_context(tc.manual_schedule())
        keep = ctx.enter_context(tc.tile_pool(name="keep", bufs=1))
        psum = ctx.enter_context(tc.psum_pool(name="psum", bufs=1))

        att_cols = keep.tile([P, 2, ATT_RUN], BF16)
        for e in range(PAIR):
            nc.sync.dma_start(
                out=att_cols[e:P:PAIR, :, :],
                in_=h_att[1:3].rearrange("i b o y x -> i (b o y x)").rearrange("i (a m) -> a i m", m=ATT_RUN),
            )
        x_sb = keep.tile([P, B, PACK, PIX], BF16)
        for b in range(B):
            nc.sync.dma_start(
                out=x_sb[:, b].rearrange("q t x -> q (t x)"),
                in_=xp[b].rearrange("(q t) y x -> q (t y x)", t=PACK),
            )
        w_sb = keep.tile([P, TILES, C], BF16)
        nc.sync.dma_start(out=w_sb[:, 0:2, :], in_=Wu.rearrange("(t p) k -> p t k", p=P))
        nc.sync.dma_start(out=w_sb[:, 2, :], in_=Wl)
        gb_rows = keep.tile([P, P], BF16)
        nc.vector.memset(gb_rows[:], 0.0)
        nc.sync.dma_start(out=gb_rows[0:2, :], in_=gamma_u.rearrange("(t p) -> t p", p=P))
        nc.sync.dma_start(out=gb_rows[2:3, :], in_=gamma_l.rearrange("(t p) -> t p", p=P))
        nc.sync.dma_start(out=gb_rows[3:5, :], in_=beta_u.rearrange("(t p) -> t p", p=P))
        nc.sync.dma_start(out=gb_rows[5:6, :], in_=beta_l.rearrange("(t p) -> t p", p=P))
        p0_sb = keep.tile([P, PIX], BF16)
        nc.sync.dma_start(out=p0_sb[:], in_=p_nodes[0].rearrange("b h y x -> (b h) (y x)"))
        h0_sb = keep.tile([P, PIX], BF16)
        nc.sync.dma_start(out=h0_sb[:], in_=h_nodes[0].rearrange("b h y x -> (b h) (y x)"))
        p_sb = keep.tile([P, TILES, B, PIX], BF16)
        for t in range(TILES):
            for j in range(NODES_PER_TILE):
                nc.sync.dma_start(
                    out=p_sb[j:P:NODES_PER_TILE, t, :, :],
                    in_=p_nodes[1 + NODES_PER_TILE * t + j].rearrange("b h y x -> h b (y x)"),
                )

        ident_bf = keep.tile([P, P], BF16)
        make_identity(nc, ident_bf[:])
        ident_f32 = keep.tile([P, P], F32)
        make_identity(nc, ident_f32[:])
        shuffle_f32 = keep.tile([P, P], F32)
        nc.gpsimd.tensor_copy(
            out=shuffle_f32[:].rearrange("p (h j) -> p h j", j=NODES_PER_TILE),
            in_=ident_f32[:].rearrange("p (j h) -> p h j", j=NODES_PER_TILE),
        )
        eps = keep.tile([P, 1], F32)
        nc.vector.memset(eps[:], EPS)
        first_call = keep.tile([P, 1], F32)
        nc.scalar.activation(out=first_call[:], in_=eps[:], func=ACT.Abs_reciprocal_sqrt)

        tiles_of = ((0, 1), (2,))
        xp_grouped = keep.tile([P, COLS, PACK], BF16)
        att_ps = [psum.tile([P, P // PAIR, ATT_RUN, PAIR], BF16, name="att_ps%d" % i) for i in range(2)]
        x_grouped = [keep.tile([P, COLS, PACK], BF16, align_bytes=64, name="x_grouped%d" % i) for i in range(2)]
        x_codes = [keep.tile([P, COLS], U32, align_bytes=64, name="x_codes%d" % i) for i in range(2)]
        x_scales = [keep.tile([P, COLS], U8, align_bytes=64, name="x_scales%d" % i) for i in range(2)]
        wT_ps = [psum.tile([P, len(tiles), 2, P], F32, name="wT_ps%d" % i) for i, tiles in enumerate(tiles_of)]
        w_grouped = keep.tile([P, TILES, P, PACK], BF16, align_bytes=64)
        w_codes = keep.tile([P, TILES, P], U32, align_bytes=64)
        w_scales = keep.tile([P, TILES, P], U8, align_bytes=64)
        y_ps = [psum.tile([P, COLS], F32, name="y_ps%d" % t) for t in tiles_of[0]]
        half_p0 = keep.tile([P, B, PIX], F32)
        stats1 = keep.tile([P, 6], F32)
        stats2 = keep.tile([P, B, 6], F32)
        mean_var = keep.tile([P, TILES, 2], F32)
        minus_mean_gamma = keep.tile([P, TILES], F32)
        rstd = keep.tile([P, TILES], F32)
        scale = keep.tile([P, TILES], F32)
        shift = keep.tile([P, TILES], F32)
        z_sb = [keep.tile([P, B, PIX], F32, name="z_sb%d" % t) for t in range(TILES)]
        o_sb = [keep.tile([P, B, PIX], F32, name="o_sb%d" % t) for t in range(TILES)]
        y0_sb = keep.tile([P, COLS], F32)
        squares = keep.tile([P, COLS], F32)
        minus_mean0 = keep.tile([P, 1], F32)
        sum_of_squares0 = keep.tile([P, 1], F32)

        def columns(b):
            return slice(b * PIX, (b + 1) * PIX)

        def tile_range(i):
            return slice(tiles_of[i][0], tiles_of[i][-1] + 1)

        def regroup_on_vector(b):
            nc.vector.tensor_copy(
                out=xp_grouped[:, columns(b), :].rearrange("q (c r) t -> q c t r", r=4),
                in_=x_sb[:, b].rearrange("q t (c r) -> q c t r", r=4),
            )

        def regroup_on_scalar_and_gpsimd(b):
            half = PIX // 2
            nc.scalar.copy(
                out=xp_grouped[:, b * PIX : b * PIX + half, :], in_=x_sb[:, b, :, 0:half].rearrange("q t x -> q x t")
            )
            nc.gpsimd.tensor_scalar(
                out=xp_grouped[:, b * PIX + half : (b + 1) * PIX, :],
                in0=x_sb[:, b, :, half:PIX].rearrange("q t x -> q x t"),
                scalar1=1.0,
                scalar2=0.0,
                op0=ALU.mult,
                op1=ALU.add,
            )

        def spread(i):
            for m in range(ATT_RUN):
                nc.tensor.transpose(
                    out=att_ps[i][:, :, m, :],
                    in_=att_cols[:, i, m : m + 1].to_broadcast([P, P]),
                    identity=ident_bf[:],
                )

        def multiply(i, b):
            nc.vector.tensor_tensor(
                out=x_grouped[i][:, columns(b), :].rearrange("q w (u e) -> q w u e", e=PAIR),
                in0=xp_grouped[:, columns(b), :].rearrange("q w (u e) -> q w u e", e=PAIR),
                in1=att_ps[i][:]
                .rearrange("q a m e -> q (a m) e")[:, columns(b), :]
                .unsqueeze(2)
                .to_broadcast([P, PIX, PACK // PAIR, PAIR]),
                op=ALU.mult,
            )

        def quantise_x(i, b):
            nc.vector.quantize_mx(
                out=x_codes[i][:, columns(b)].bitcast(FP8X4),
                scales=x_scales[i][:, columns(b)],
                in_=x_grouped[i][:, columns(b), :].rearrange("q w t -> q (w t)"),
            )

        def transpose_weights(i):
            for k, t in enumerate(tiles_of[i]):
                words = w_sb[:, t, :].bitcast(F32)
                for u in range(2):
                    nc.tensor.transpose(
                        out=wT_ps[i][:, k, u, :], in_=words[:, u : 2 * P : 2], identity=shuffle_f32[:]
                    )
            nc.scalar.copy(
                out=w_grouped[:, tile_range(i)]
                .rearrange("q k o t -> q k (o t)")
                .bitcast(F32)
                .rearrange("q k (o u) -> q k o u", u=2),
                in_=wT_ps[i][:].rearrange("q k u o -> q k o u"),
            )

        def quantise_weights(i):
            nc.vector.quantize_mx(
                out=w_codes[:, tile_range(i)].rearrange("q k o -> q (k o)").bitcast(FP8X4),
                scales=w_scales[:, tile_range(i)].rearrange("q k o -> q (k o)"),
                in_=w_grouped[:, tile_range(i)].rearrange("q k o t -> q (k o t)"),
            )

        def convolve_upper():
            for t in tiles_of[0]:
                nc.tensor.matmul_mx(
                    out=y_ps[t][:],
                    lhsT=w_codes[:, t, :].bitcast(FP8X4),
                    lhsT_scale=w_scales[:, t, :],
                    rhs=x_codes[0][:].bitcast(FP8X4),
                    rhs_scale=x_scales[0][:],
                    start=True,
                    stop=True,
                )

        def convolve_lower(b):
            nc.tensor.matmul_mx(
                out=y2_ps[b][:],
                lhsT=w_codes[:, 2, :].bitcast(FP8X4),
                lhsT_scale=w_scales[:, 2, :],
                rhs=x_codes[1][:, columns(b)].bitcast(FP8X4),
                rhs_scale=x_scales[1][:, columns(b)],
                start=True,
                stop=True,
            )

        def statistics_on_scalar():
            nc.scalar.activation(
                out=y0_sb[:], in_=y_ps[0][:], func=ACT.Copy, scale=-1.0 / COLS, accum_out=minus_mean0[:]
            )
            nc.scalar.activation(
                out=squares[:], in_=y_ps[0][:], func=ACT.Square, bias=minus_mean0[:], accum_out=sum_of_squares0[:]
            )
            nc.scalar.activation(
                out=minus_mean_gamma[:, 0:1], in_=minus_mean0[:], func=ACT.Copy, scale=half_gb[:, 0, 0:1]
            )
            nc.scalar.activation(
                out=rstd[:, 0:1],
                in_=sum_of_squares0[:],
                func=ACT.Abs_reciprocal_sqrt,
                scale=1.0 / COLS,
                bias=eps[:],
            )

        def root(t):
            nc.scalar.activation(
                out=rstd[:, t : t + 1], in_=mean_var[:, t, 1:2], func=ACT.Abs_reciprocal_sqrt, bias=eps[:]
            )
            nc.scalar.activation(
                out=minus_mean_gamma[:, t : t + 1],
                in_=mean_var[:, t, 0:1],
                func=ACT.Copy,
                scale=minus_half_gamma[:, t : t + 1],
            )

        def scale_and_shift(t):
            nc.scalar.activation(
                out=scale[:, t : t + 1],
                in_=rstd[:, t : t + 1],
                func=ACT.Copy,
                scale=gamma_for_y0_sb[:] if t == 0 else half_gb[:, 0, t : t + 1],
            )
            nc.scalar.activation(
                out=shift[:, t : t + 1],
                in_=minus_mean_gamma[:, t : t + 1],
                func=ACT.Identity,
                scale=rstd[:, t : t + 1],
                bias=half_gb[:, 1, t : t + 1],
            )

        def normalise_on_scalar(t, z, y):
            nc.scalar.activation(
                out=z, in_=y, func=ACT.Relu, bias=shift[:, t : t + 1], scale=scale[:, t : t + 1]
            )

        def normalise_on_vector(t):
            nc.vector.tensor_scalar(
                out=z_sb[t][:].rearrange("p b x -> p (b x)"),
                in0=y0_sb[:],
                scalar1=scale[:, t : t + 1],
                scalar2=shift[:, t : t + 1],
                op0=ALU.mult,
                op1=ALU.add,
            )

        def store(t, images):
            queues = (nc.sync, nc.scalar) if t == 2 else (nc.sync, nc.sync)
            for j in range(NODES_PER_TILE):
                queues[j].dma_start(
                    out=out[1 + NODES_PER_TILE * t + j].rearrange("b h y x -> h b (y x)")[:, images, :],
                    in_=o_sb[t][j:P:NODES_PER_TILE, images, :],
                )

        def relu_average_store(t):
            nc.vector.scalar_tensor_tensor(
                out=o_sb[t][:], in0=z_sb[t][:], scalar=0.0, in1=half_p0[:], op0=ALU.max, op1=ALU.add
            )
            store(t, slice(0, B))

        def average_store(t, images):
            nc.vector.scalar_tensor_tensor(
                out=o_sb[t][:, images, :],
                in0=p_sb[:, t, images, :],
                scalar=0.5,
                in1=z_sb[t][:, images, :],
                op0=ALU.mult,
                op1=ALU.add,
            )
            store(t, images)

        regroup_on_scalar_and_gpsimd(1)
        spread(0)
        spread(1)
        transpose_weights(0)
        transpose_weights(1)

        gb_shuffled = keep.tile([P, P], BF16)
        nc.gpsimd.tensor_copy(
            out=gb_shuffled[:].rearrange("r (h j) -> r h j", j=NODES_PER_TILE),
            in_=gb_rows[:].rearrange("r (j h) -> r h j", j=NODES_PER_TILE),
        )
        gbT_ps = psum.tile([P, P], BF16, tag="small")
        nc.tensor.transpose(out=gbT_ps[:], in_=gb_shuffled[:], identity=ident_bf[:])
        half_gb = keep.tile([P, 2, TILES], F32)
        nc.scalar.mul(
            out=half_gb[:].rearrange("p g t -> p (g t)"), in_=gbT_ps[:, 0 : 2 * TILES], mul=0.5
        )
        minus_half_gamma = keep.tile([P, TILES], F32)
        nc.scalar.mul(out=minus_half_gamma[:], in_=gbT_ps[:, 0:TILES], mul=-0.5)
        gamma_for_y0_sb = keep.tile([P, 1], F32)
        nc.scalar.mul(out=gamma_for_y0_sb[:], in_=gbT_ps[:, 0:1], mul=-0.5 * COLS)
        o0_sb = keep.tile([P, PIX], F32)
        nc.gpsimd.tensor_tensor(out=o0_sb[:], in0=p0_sb[:], in1=h0_sb[:], op=ALU.add)
        nc.scalar.mul(out=o0_sb[:], in_=o0_sb[:], mul=0.5)
        nc.sync.dma_start(out=out[0].rearrange("b h y x -> (b h) (y x)"), in_=o0_sb[:])
        nc.scalar.mul(out=half_p0[:], in_=p_sb[:, 0], mul=0.5)

        y2_ps = [psum.tile([P, PIX], F32, name="y2_ps0"), psum.tile([P, PIX], F32, tag="small", name="y2_ps1")]

        regroup_on_vector(0)
        multiply(0, 0)
        multiply(1, 0)
        multiply(0, 1)
        for b in range(B):
            quantise_x(0, b)
        quantise_weights(0)
        convolve_upper()
        statistics_on_scalar()
        multiply(1, 1)
        quantise_weights(1)
        for b in range(B):
            quantise_x(1, b)
            convolve_lower(b)

        both = slice(0, B)
        nc.vector.bn_stats(out=stats1[:], in_=y_ps[1][:])
        nc.vector.bn_stats(out=stats2[:, 0, :], in_=y2_ps[0][:])
        nc.vector.bn_aggr(out=mean_var[:, 1, :], in_=stats1[:])
        nc.vector.bn_stats(out=stats2[:, 1, :], in_=y2_ps[1][:])
        nc.vector.bn_aggr(out=mean_var[:, 2, :], in_=stats2[:].rearrange("p b s -> p (b s)"))
        root(1)
        scale_and_shift(0)
        scale_and_shift(1)
        normalise_on_vector(0)
        root(2)
        normalise_on_scalar(1, z_sb[1][:].rearrange("p b x -> p (b x)"), y_ps[1][:])
        scale_and_shift(2)
        relu_average_store(0)
        average_store(1, both)
        for b in range(B):
            normalise_on_scalar(2, z_sb[2][:, b, :], y2_ps[b][:])
        for b in range(B):
            average_store(2, slice(b, b + 1))
